import numpy as np
import ml_dtypes


def mxq(x, axis, fmt="e4m3"):
    dtype, down = {"e4m3": (ml_dtypes.float8_e4m3fn, 7), "e5m2": (ml_dtypes.float8_e5m2, 14)}[fmt]
    v = np.moveaxis(np.asarray(x, np.float32).astype(ml_dtypes.bfloat16).astype(np.float64), axis, -1)
    blocks = v.reshape(v.shape[:-1] + (-1, 32))
    amax = np.abs(blocks).max(-1, keepdims=True)
    byte = np.maximum(np.where(amax > 0, np.frexp(amax)[1] - 1 + 127, 0) - down, 1)
    scale = np.exp2(byte - 127.0)
    codes = (blocks / scale).astype(np.float32).astype(dtype).astype(np.float64)
    return np.moveaxis((codes * scale).reshape(v.shape), -1, axis)


WIDE = False


def mx_kscale(k):
    if not WIDE:
        return np.ones(k)
    levels = np.array([10, -10, 5, -5, 0])
    a = np.random.permutation(np.resize(levels, k // 512 * 4)).reshape(k // 512, 4)
    idx = np.arange(k)
    return np.exp2(a[idx // 512, idx % 128 // 32])


BF16 = ml_dtypes.bfloat16


def bf(x):
    return np.asarray(x, np.float32).astype(BF16)


def f64(x):
    return np.asarray(x).astype(np.float64)


B, T, S, Dt, Df = 2, 512, 512, 2048, 2048
EPS = 1e-6


def rmsnorm(x, w):
    return x * (1.0 / np.sqrt(np.mean(x * x, axis=-1, keepdims=True) + EPS)) * w


def setup_inputs():
    s = mx_kscale(Dt)
    t = mx_kscale(Df)
    return {"text": bf(np.random.standard_normal((B, T, Dt)) * s),
            "Wq_w": bf(np.random.standard_normal((Df, Dt)) / np.sqrt(Dt) / s[None, :]),
            "Wq_b": bf(np.random.standard_normal(Df) * 0.3),
            "qn_w": bf((1.0 + 0.1 * np.random.standard_normal(Df)) * t),
            "k_norm": bf(np.random.standard_normal((B, S, Df)) / t)}


def reference(text, Wq_w, Wq_b, qn_w, k_norm):
    q = (mxq(f64(text), 2, "e4m3") @ mxq(f64(Wq_w), 1, "e4m3").T) + f64(Wq_b)
    q = rmsnorm(q, f64(qn_w))
    scale = 1.0 / np.sqrt(Df)
    return (mxq(q, 2, "e4m3") @ mxq(f64(k_norm), 2, "e4m3").transpose(0, 2, 1)) * scale

@@ -1,0 +1,276 @@
+from contextlib import ExitStack
+
+import concourse.mybir as mybir
+from concourse.masks import make_identity
+
+F32 = mybir.dt.float32
+BF16 = mybir.dt.bfloat16
+U32 = mybir.dt.uint32
+U8 = mybir.dt.uint8
+FP8X4 = mybir.dt.float8_e4m3fn_x4
+ACT = mybir.ActivationFunctionType
+ALU = mybir.AluOpType
+
+P = 128
+D = 2048
+PASSES = 4
+TOKENS = 1024
+BLOCK = 512
+UNIT_ROWS = 256
+W_UNITS = D // UNIT_ROWS
+EPS = 1e-6
+SCORE_SCALE = 1.0 / (2048.0 ** 0.5)
+
+FLOPS = 2 * TOKENS * D * D + 2 * TOKENS * BLOCK * D
+
+RAW_BUFS = 4
+LEAD = 4
+
+
+def tile_crossattention_pb_kernel(tc, text, Wq_w, Wq_b, qn_w, k_norm, out):
+    nc = tc.nc
+    text_rows = text.flatten_outer_dims()
+    key_rows = k_norm.flatten_outer_dims()
+    out_rows = out.flatten_outer_dims()
+
+    units = [("text", 0), ("text", 1)]
+    units += [("weights", m) for m in range(W_UNITS)]
+    units += [("text", 2), ("text", 3)]
+    units += [("keys", h) for h in range(4)]
+
+    with ExitStack() as ctx:
+        consts = ctx.enter_context(tc.tile_pool(name="consts", bufs=1))
+        codes = ctx.enter_context(tc.tile_pool(name="codes", bufs=1))
+        raw_pool = ctx.enter_context(tc.tile_pool(name="raw", bufs=RAW_BUFS))
+        grouped_pool = ctx.enter_context(tc.tile_pool(name="grouped", bufs=3))
+        y_pool = ctx.enter_context(tc.tile_pool(name="y", bufs=5))
+        q_pool = ctx.enter_context(tc.tile_pool(name="q", bufs=2))
+        sq_pool = ctx.enter_context(tc.tile_pool(name="sq", bufs=3))
+        norm_pool = ctx.enter_context(tc.tile_pool(name="norm", bufs=2))
+        o_pool = ctx.enter_context(tc.tile_pool(name="o", bufs=3))
+        psum = ctx.enter_context(tc.psum_pool(name="psum", bufs=4))
+        ctx.enter_context(tc.manual_schedule())
+
+        def load_unit(n):
+            kind, index = units[n]
+            rows = slice(index * UNIT_ROWS, (index + 1) * UNIT_ROWS)
+            raw = raw_pool.tile([P, 2 * D], BF16, name="raw")
+            if kind == "weights":
+                view = Wq_w[rows, :].rearrange("(p e) k -> p e k", e=2)
+            elif kind == "text":
+                view = text_rows[rows, :].rearrange("(e p) k -> p e k", e=2)
+            else:
+                view = key_rows[rows, :].rearrange("(e p) k -> p e k", e=2)
+            nc.sync.dma_start(out=raw[:].rearrange("p (e k) -> p e k", e=2), in_=view)
+            return raw
+
+        vec_rows = consts.tile([P, 2 * P], BF16, name="vec_rows")
+        nc.vector.memset(vec_rows[:], 0.0)
+        nc.scalar.dma_start(out=vec_rows[0:8, :], in_=Wq_b.rearrange("(m c) -> m c", m=8))
+        nc.scalar.dma_start(out=vec_rows[8:16, :], in_=qn_w.rearrange("(m c) -> m c", m=8))
+
+        raw_of = {}
+        for n in range(RAW_BUFS):
+            raw_of[n] = load_unit(n)
+
+        ident = consts.tile([P, P], F32, name="ident")
+        make_identity(nc, ident[:])
+        mean_w = consts.tile([P, P], F32, name="mean_w")
+        nc.vector.memset(mean_w[:], 1.0 / D)
+        eps = consts.tile([P, 1], F32, name="eps")
+        nc.vector.memset(eps[:], EPS)
+        warm = consts.tile([P, 1], F32, name="warm")
+        nc.scalar.activation(out=warm[:], in_=eps[:], func=ACT.Abs_reciprocal_sqrt)
+
+        bias_gain = consts.tile([P, 32], F32, name="bias_gain")
+        bias = bias_gain[:, 0:16]
+        gain = bias_gain[:, 16:32]
+        gain_bias = consts.tile([P, 16], F32, name="gain_bias")
+
+        def spread_bias_and_gain():
+            vec_bank = psum.tile([P, 2, 2, P], F32, name="tp")
+            nc.tensor.transpose(vec_bank[:, 0, 0, :], vec_rows[:].bitcast(F32), ident[:])
+            nc.vector.tensor_copy(out=bias_gain[:], in_=vec_bank[:, 0, 0, 0:16].bitcast(BF16))
+            nc.vector.tensor_tensor(out=gain_bias[:], in0=gain, in1=bias, op=ALU.mult)
+
+        w_codes = []
+        w_scales = []
+        for m in range(W_UNITS):
+            w_codes.append(codes.tile([P, 2 * PASSES * P], U32, name="w_codes%d" % m, align_bytes=64))
+            w_scales.append(codes.tile([P, 2 * PASSES * P], U8, name="w_scales%d" % m, align_bytes=64))
+        text_codes = codes.tile([P, PASSES, TOKENS], U32, name="text_codes", align_bytes=64)
+        text_scales = codes.tile([P, PASSES, TOKENS], U8, name="text_scales", align_bytes=64)
+        key_codes = codes.tile([P, PASSES, TOKENS], U32, name="key_codes", align_bytes=64)
+        key_scales = codes.tile([P, PASSES, TOKENS], U8, name="key_scales", align_bytes=64)
+        q_codes = codes.tile([P, PASSES, TOKENS], U32, name="q_codes", align_bytes=64)
+        q_scales = codes.tile([P, PASSES, TOKENS], U8, name="q_scales", align_bytes=64)
+
+        def transpose_unit(n):
+            kind, index = units[n]
+            words = raw_of[n][:].bitcast(F32).rearrange(
+                "p (e g u c) -> p e g u c", e=2, g=PASSES, u=2
+            )
+            grouped = grouped_pool.tile([P, 2 * D], BF16, name="grouped", align_bytes=64)
+            grouped_words = grouped[:].bitcast(F32).rearrange(
+                "p (a x r u) -> p a x r u", a=4, x=2, u=2
+            )
+            for a in range(4):
+                bank = psum.tile([P, 2, 2, P], F32, name="tp")
+                for x in range(2):
+                    if kind == "weights":
+                        e, g = a // 2, 2 * (a % 2) + x
+                    else:
+                        e, g = x, a
+                    for u in range(2):
+                        nc.tensor.transpose(bank[:, x, u, :], words[:, e, g, u, :], ident[:])
+                nc.scalar.copy(
+                    out=grouped_words[:, a], in_=bank[:].rearrange("p x u r -> p x r u")
+                )
+            return grouped
+
+        def quantise_unit(n, grouped):
+            kind, index = units[n]
+            if kind == "weights":
+                nc.vector.quantize_mx(
+                    out=w_codes[index][:].bitcast(FP8X4), scales=w_scales[index][:], in_=grouped[:]
+                )
+                return
+            dst_codes, dst_scales = (text_codes, text_scales) if kind == "text" else (key_codes, key_scales)
+            cols = slice(index * UNIT_ROWS, (index + 1) * UNIT_ROWS)
+            for g in range(PASSES):
+                nc.vector.quantize_mx(
+                    out=dst_codes[:, g, cols].bitcast(FP8X4),
+                    scales=dst_scales[:, g, cols],
+                    in_=grouped[:, g * 4 * UNIT_ROWS : (g + 1) * 4 * UNIT_ROWS],
+                )
+
+        y_of = {}
+        acc_of = {}
+        inv_of = {}
+
+        def project(block, m):
+            tokens = slice(block * BLOCK, (block + 1) * BLOCK)
+            for e in range(2):
+                j = 2 * m + e
+                bank = psum.tile([P, BLOCK], F32, name="mm")
+                for g in range(PASSES):
+                    cols = slice((PASSES * e + g) * P, (PASSES * e + g + 1) * P)
+                    nc.tensor.matmul_mx(
+                        out=bank[:],
+                        lhsT=w_codes[m][:, cols].bitcast(FP8X4),
+                        lhsT_scale=w_scales[m][:, cols],
+                        rhs=text_codes[:, g, tokens].bitcast(FP8X4),
+                        rhs_scale=text_scales[:, g, tokens],
+                        start=(g == 0),
+                        stop=(g == PASSES - 1),
+                    )
+                if j % 4 == 0:
+                    y_of[(block, j // 4)] = y_pool.tile([P, 4, BLOCK], F32, name="y4")
+                y4 = y_of[(block, j // 4)]
+                if j == 0:
+                    acc_of[block] = norm_pool.tile([P, BLOCK], F32, name="acc")
+                    sq = acc_of[block]
+                else:
+                    sq = sq_pool.tile([P, BLOCK], F32, name="sq")
+                nc.scalar.activation(
+                    out=sq[:], in_=bank[:], func=ACT.Square, bias=bias[:, j : j + 1], scale=1.0
+                )
+                if block == 0:
+                    nc.vector.tensor_scalar(
+                        out=y4[:, j % 4, :],
+                        in0=bank[:],
+                        scalar1=gain[:, j : j + 1],
+                        scalar2=gain_bias[:, j : j + 1],
+                        op0=ALU.mult,
+                        op1=ALU.add,
+                    )
+                else:
+                    nc.scalar.activation(
+                        out=y4[:, j % 4, :],
+                        in_=bank[:],
+                        func=ACT.Identity,
+                        bias=gain_bias[:, j : j + 1],
+                        scale=gain[:, j : j + 1],
+                    )
+                if j > 0:
+                    acc = acc_of[block]
+                    nc.vector.tensor_tensor(out=acc[:], in0=acc[:], in1=sq[:], op=ALU.add)
+
+        def rms_factor(block):
+            bank = psum.tile([P, BLOCK], F32, name="mm")
+            nc.tensor.matmul(out=bank[:], lhsT=mean_w[:], rhs=acc_of[block][:], start=True, stop=True)
+            inv = norm_pool.tile([P, BLOCK], F32, name="inv")
+            nc.scalar.activation(
+                out=inv[:], in_=bank[:], func=ACT.Abs_reciprocal_sqrt, bias=eps[:, 0:1], scale=1.0
+            )
+            inv_of[block] = inv
+
+        def normalise(block, g):
+            tokens = slice(block * BLOCK, (block + 1) * BLOCK)
+            q_grouped = q_pool.tile([P, 4 * BLOCK], BF16, name="q_grouped", align_bytes=64)
+            nc.vector.tensor_tensor(
+                out=q_grouped[:].rearrange("p (n t) -> p n t", t=4),
+                in0=y_of[(block, g)][:].rearrange("p t n -> p n t"),
+                in1=inv_of[block][:].unsqueeze(2).to_broadcast([P, BLOCK, 4]),
+                op=ALU.mult,
+            )
+            nc.vector.quantize_mx(
+                out=q_codes[:, g, tokens].bitcast(FP8X4),
+                scales=q_scales[:, g, tokens],
+                in_=q_grouped[:],
+            )
+
+        def score_pass(block, g, banks):
+            keys = slice(block * BLOCK, (block + 1) * BLOCK)
+            for i in range(4):
+                tokens = slice(block * BLOCK + i * P, block * BLOCK + (i + 1) * P)
+                nc.tensor.matmul_mx(
+                    out=banks[i][:],
+                    lhsT=q_codes[:, g, tokens].bitcast(FP8X4),
+                    lhsT_scale=q_scales[:, g, tokens],
+                    rhs=key_codes[:, g, keys].bitcast(FP8X4),
+                    rhs_scale=key_scales[:, g, keys],
+                    start=(g == 0),
+                    stop=(g == PASSES - 1),
+                )
+
+        def store_scores(block, banks):
+            for i in range(4):
+                o_sb = o_pool.tile([P, BLOCK], F32, name="o_sb")
+                if block == 1 and i % 2 == 1:
+                    nc.vector.tensor_scalar_mul(out=o_sb[:], in0=banks[i][:], scalar1=SCORE_SCALE)
+                else:
+                    nc.scalar.activation(
+                        out=o_sb[:], in_=banks[i][:], func=ACT.Copy, scale=SCORE_SCALE
+                    )
+                rows = slice(block * BLOCK + i * P, block * BLOCK + (i + 1) * P)
+                nc.sync.dma_start(out=out_rows[rows, :], in_=o_sb[:])
+
+        grouped_of = {}
+        for n in range(len(units) + LEAD):
+            if n < len(units):
+                grouped_of[n] = transpose_unit(n)
+                if n + RAW_BUFS < len(units):
+                    raw_of[n + RAW_BUFS] = load_unit(n + RAW_BUFS)
+            if 1 <= n <= len(units):
+                quantise_unit(n - 1, grouped_of[n - 1])
+            if n == 1:
+                spread_bias_and_gain()
+            if n >= LEAD:
+                block, m = divmod(n - LEAD, W_UNITS)
+                project(block, m)
+                if block == 1 and m == 0:
+                    rms_factor(0)
+                if block == 1 and m % 2 == 0:
+                    normalise(0, m // 2)
+
+        rms_factor(1)
+        banks0 = [psum.tile([P, BLOCK], F32, name="sc%d" % i, tag="tp") for i in range(4)]
+        for g in range(PASSES):
+            score_pass(0, g, banks0)
+        store_scores(0, banks0)
+        banks1 = [psum.tile([P, BLOCK], F32, name="sd%d" % i, tag="mm") for i in range(4)]
+        for g in range(PASSES):
+            normalise(1, g)
+            score_pass(1, g, banks1)
+        store_scores(1, banks1)

@@ -123,9 +123,14 @@ def tile_crossattention_pb_kernel(tc, text, Wq_w, Wq_b, qn_w, k_norm, out):
                         e, g = x, a
                     for u in range(2):
                         nc.tensor.transpose(bank[:, x, u, :], words[:, e, g, u, :], ident[:])
-                nc.scalar.copy(
-                    out=grouped_words[:, a], in_=bank[:].rearrange("p x u r -> p x r u")
-                )
+                if kind == "weights" and a == 3:
+                    nc.vector.tensor_copy(
+                        out=grouped_words[:, a], in_=bank[:].rearrange("p x u r -> p x r u")
+                    )
+                else:
+                    nc.scalar.copy(
+                        out=grouped_words[:, a], in_=bank[:].rearrange("p x u r -> p x r u")
+                    )
             return grouped
 
         def quantise_unit(n, grouped):
@@ -175,26 +180,17 @@ def tile_crossattention_pb_kernel(tc, text, Wq_w, Wq_b, qn_w, k_norm, out):
                 nc.scalar.activation(
                     out=sq[:], in_=bank[:], func=ACT.Square, bias=bias[:, j : j + 1], scale=1.0
                 )
-                if block == 0:
-                    nc.vector.tensor_scalar(
-                        out=y4[:, j % 4, :],
-                        in0=bank[:],
-                        scalar1=gain[:, j : j + 1],
-                        scalar2=gain_bias[:, j : j + 1],
-                        op0=ALU.mult,
-                        op1=ALU.add,
-                    )
-                else:
-                    nc.scalar.activation(
-                        out=y4[:, j % 4, :],
-                        in_=bank[:],
-                        func=ACT.Identity,
-                        bias=gain_bias[:, j : j + 1],
-                        scale=gain[:, j : j + 1],
-                    )
+                nc.vector.tensor_scalar(
+                    out=y4[:, j % 4, :],
+                    in0=bank[:],
+                    scalar1=gain[:, j : j + 1],
+                    scalar2=gain_bias[:, j : j + 1],
+                    op0=ALU.mult,
+                    op1=ALU.add,
+                )
                 if j > 0:
                     acc = acc_of[block]
-                    nc.vector.tensor_tensor(out=acc[:], in0=acc[:], in1=sq[:], op=ALU.add)
+                    nc.gpsimd.tensor_tensor(out=acc[:], in0=acc[:], in1=sq[:], op=ALU.add)
 
         def rms_factor(block):
             bank = psum.tile([P, BLOCK], F32, name="mm")
@@ -248,12 +244,12 @@ def tile_crossattention_pb_kernel(tc, text, Wq_w, Wq_b, qn_w, k_norm, out):
 
         grouped_of = {}
         for n in range(len(units) + LEAD):
+            if 1 <= n <= len(units):
+                quantise_unit(n - 1, grouped_of[n - 1])
             if n < len(units):
                 grouped_of[n] = transpose_unit(n)
                 if n + RAW_BUFS < len(units):
                     raw_of[n + RAW_BUFS] = load_unit(n + RAW_BUFS)
-            if 1 <= n <= len(units):
-                quantise_unit(n - 1, grouped_of[n - 1])
             if n == 1:
                 spread_bias_and_gain()
             if n >= LEAD:

@@ -123,14 +123,9 @@ def tile_crossattention_pb_kernel(tc, text, Wq_w, Wq_b, qn_w, k_norm, out):
                         e, g = x, a
                     for u in range(2):
                         nc.tensor.transpose(bank[:, x, u, :], words[:, e, g, u, :], ident[:])
-                if kind == "weights" and a == 3:
-                    nc.vector.tensor_copy(
-                        out=grouped_words[:, a], in_=bank[:].rearrange("p x u r -> p x r u")
-                    )
-                else:
-                    nc.scalar.copy(
-                        out=grouped_words[:, a], in_=bank[:].rearrange("p x u r -> p x r u")
-                    )
+                nc.scalar.copy(
+                    out=grouped_words[:, a], in_=bank[:].rearrange("p x u r -> p x r u")
+                )
             return grouped
 
         def quantise_unit(n, grouped):
@@ -180,17 +175,26 @@ def tile_crossattention_pb_kernel(tc, text, Wq_w, Wq_b, qn_w, k_norm, out):
                 nc.scalar.activation(
                     out=sq[:], in_=bank[:], func=ACT.Square, bias=bias[:, j : j + 1], scale=1.0
                 )
-                nc.vector.tensor_scalar(
-                    out=y4[:, j % 4, :],
-                    in0=bank[:],
-                    scalar1=gain[:, j : j + 1],
-                    scalar2=gain_bias[:, j : j + 1],
-                    op0=ALU.mult,
-                    op1=ALU.add,
-                )
+                if block == 0:
+                    nc.vector.tensor_scalar(
+                        out=y4[:, j % 4, :],
+                        in0=bank[:],
+                        scalar1=gain[:, j : j + 1],
+                        scalar2=gain_bias[:, j : j + 1],
+                        op0=ALU.mult,
+                        op1=ALU.add,
+                    )
+                else:
+                    nc.scalar.activation(
+                        out=y4[:, j % 4, :],
+                        in_=bank[:],
+                        func=ACT.Identity,
+                        bias=gain_bias[:, j : j + 1],
+                        scale=gain[:, j : j + 1],
+                    )
                 if j > 0:
                     acc = acc_of[block]
-                    nc.gpsimd.tensor_tensor(out=acc[:], in0=acc[:], in1=sq[:], op=ALU.add)
+                    nc.vector.tensor_tensor(out=acc[:], in0=acc[:], in1=sq[:], op=ALU.add)
 
         def rms_factor(block):
             bank = psum.tile([P, BLOCK], F32, name="mm")
@@ -205,9 +209,12 @@ def tile_crossattention_pb_kernel(tc, text, Wq_w, Wq_b, qn_w, k_norm, out):
             tokens = slice(block * BLOCK, (block + 1) * BLOCK)
             q_grouped = q_pool.tile([P, 4 * BLOCK], BF16, name="q_grouped", align_bytes=64)
             nc.vector.tensor_tensor(
-                out=q_grouped[:].rearrange("p (n t) -> p n t", t=4),
-                in0=y_of[(block, g)][:].rearrange("p t n -> p n t"),
-                in1=inv_of[block][:].unsqueeze(2).to_broadcast([P, BLOCK, 4]),
+                out=q_grouped[:].rearrange("p (c i t) -> p c t i", i=4, t=4),
+                in0=y_of[(block, g)][:].rearrange("p t (c i) -> p c t i", i=4),
+                in1=inv_of[block][:]
+                .rearrange("p (c i) -> p c i", i=4)
+                .unsqueeze(2)
+                .to_broadcast([P, BLOCK // 4, 4, 4]),
                 op=ALU.mult,
             )
             nc.vector.quantize_mx(
@@ -244,12 +251,12 @@ def tile_crossattention_pb_kernel(tc, text, Wq_w, Wq_b, qn_w, k_norm, out):
 
         grouped_of = {}
         for n in range(len(units) + LEAD):
-            if 1 <= n <= len(units):
-                quantise_unit(n - 1, grouped_of[n - 1])
             if n < len(units):
                 grouped_of[n] = transpose_unit(n)
                 if n + RAW_BUFS < len(units):
                     raw_of[n + RAW_BUFS] = load_unit(n + RAW_BUFS)
+            if 1 <= n <= len(units):
+                quantise_unit(n - 1, grouped_of[n - 1])
             if n == 1:
                 spread_bias_and_gain()
             if n >= LEAD:

@@ -37,6 +37,7 @@ def tile_crossattention_pb_kernel(tc, text, Wq_w, Wq_b, qn_w, k_norm, out):
     units += [("weights", m) for m in range(W_UNITS)]
     units += [("text", 2), ("text", 3)]
     units += [("keys", h) for h in range(4)]
+    FIRST_KEYS = len(units) - 4
 
     with ExitStack() as ctx:
         consts = ctx.enter_context(tc.tile_pool(name="consts", bufs=1))
@@ -250,13 +251,14 @@ def tile_crossattention_pb_kernel(tc, text, Wq_w, Wq_b, qn_w, k_norm, out):
                 nc.sync.dma_start(out=out_rows[rows, :], in_=o_sb[:])
 
         grouped_of = {}
-        for n in range(len(units) + LEAD):
-            if n < len(units):
-                grouped_of[n] = transpose_unit(n)
-                if n + RAW_BUFS < len(units):
-                    raw_of[n + RAW_BUFS] = load_unit(n + RAW_BUFS)
-            if 1 <= n <= len(units):
+        for n in range(2 * W_UNITS + LEAD):
+            if 1 <= n <= FIRST_KEYS and units[n - 1][0] == "weights":
                 quantise_unit(n - 1, grouped_of[n - 1])
+            if n < FIRST_KEYS:
+                grouped_of[n] = transpose_unit(n)
+                raw_of[n + RAW_BUFS] = load_unit(n + RAW_BUFS)
+                if units[n][0] == "text":
+                    quantise_unit(n, grouped_of[n])
             if n == 1:
                 spread_bias_and_gain()
             if n >= LEAD:
@@ -267,13 +269,19 @@ def tile_crossattention_pb_kernel(tc, text, Wq_w, Wq_b, qn_w, k_norm, out):
                 if block == 1 and m % 2 == 0:
                     normalise(0, m // 2)
 
+        grouped_of[FIRST_KEYS] = transpose_unit(FIRST_KEYS)
         rms_factor(1)
-        banks0 = [psum.tile([P, BLOCK], F32, name="sc%d" % i, tag="tp") for i in range(4)]
         for g in range(PASSES):
-            score_pass(0, g, banks0)
-        store_scores(0, banks0)
-        banks1 = [psum.tile([P, BLOCK], F32, name="sd%d" % i, tag="mm") for i in range(4)]
-        for g in range(PASSES):
+            if g + 1 < 4:
+                grouped_of[FIRST_KEYS + g + 1] = transpose_unit(FIRST_KEYS + g + 1)
+            quantise_unit(FIRST_KEYS + g, grouped_of[FIRST_KEYS + g])
+            if g == 2:
+                banks0 = [psum.tile([P, BLOCK], F32, name="sc%d" % i, tag="mm") for i in range(4)]
+                for gg in range(PASSES):
+                    score_pass(0, gg, banks0)
+                store_scores(0, banks0)
             normalise(1, g)
+        banks1 = [psum.tile([P, BLOCK], F32, name="sd%d" % i, tag="tp") for i in range(4)]
+        for g in range(PASSES):
             score_pass(1, g, banks1)
         store_scores(1, banks1)

@@ -50,7 +50,6 @@ def tile_crossattention_pb_kernel(tc, text, Wq_w, Wq_b, qn_w, k_norm, out):
         norm_pool = ctx.enter_context(tc.tile_pool(name="norm", bufs=2))
         o_pool = ctx.enter_context(tc.tile_pool(name="o", bufs=3))
         psum = ctx.enter_context(tc.psum_pool(name="psum", bufs=4))
-        ctx.enter_context(tc.manual_schedule())
 
         def load_unit(n):
             kind, index = units[n]

@@ -46,7 +46,7 @@ def tile_crossattention_pb_kernel(tc, text, Wq_w, Wq_b, qn_w, k_norm, out):
         grouped_pool = ctx.enter_context(tc.tile_pool(name="grouped", bufs=3))
         y_pool = ctx.enter_context(tc.tile_pool(name="y", bufs=5))
         q_pool = ctx.enter_context(tc.tile_pool(name="q", bufs=2))
-        sq_pool = ctx.enter_context(tc.tile_pool(name="sq", bufs=3))
+        sq_pool = ctx.enter_context(tc.tile_pool(name="sq", bufs=6))
         norm_pool = ctx.enter_context(tc.tile_pool(name="norm", bufs=2))
         o_pool = ctx.enter_context(tc.tile_pool(name="o", bufs=3))
         psum = ctx.enter_context(tc.psum_pool(name="psum", bufs=4))
@@ -175,23 +175,14 @@ def tile_crossattention_pb_kernel(tc, text, Wq_w, Wq_b, qn_w, k_norm, out):
                 nc.scalar.activation(
                     out=sq[:], in_=bank[:], func=ACT.Square, bias=bias[:, j : j + 1], scale=1.0
                 )
-                if block == 0:
-                    nc.vector.tensor_scalar(
-                        out=y4[:, j % 4, :],
-                        in0=bank[:],
-                        scalar1=gain[:, j : j + 1],
-                        scalar2=gain_bias[:, j : j + 1],
-                        op0=ALU.mult,
-                        op1=ALU.add,
-                    )
-                else:
-                    nc.scalar.activation(
-                        out=y4[:, j % 4, :],
-                        in_=bank[:],
-                        func=ACT.Identity,
-                        bias=gain_bias[:, j : j + 1],
-                        scale=gain[:, j : j + 1],
-                    )
+                nc.any.tensor_scalar(
+                    out=y4[:, j % 4, :],
+                    in0=bank[:],
+                    scalar1=gain[:, j : j + 1],
+                    scalar2=gain_bias[:, j : j + 1],
+                    op0=ALU.mult,
+                    op1=ALU.add,
+                )
                 if j > 0:
                     acc = acc_of[block]
                     nc.vector.tensor_tensor(out=acc[:], in0=acc[:], in1=sq[:], op=ALU.add)
@@ -205,9 +196,11 @@ def tile_crossattention_pb_kernel(tc, text, Wq_w, Wq_b, qn_w, k_norm, out):
             )
             inv_of[block] = inv
 
-        def normalise(block, g):
-            tokens = slice(block * BLOCK, (block + 1) * BLOCK)
+        q_grouped_of = {}
+
+        def scale_queries(block, g):
             q_grouped = q_pool.tile([P, 4 * BLOCK], BF16, name="q_grouped", align_bytes=64)
+            q_grouped_of[(block, g)] = q_grouped
             nc.vector.tensor_tensor(
                 out=q_grouped[:].rearrange("p (c i t) -> p c t i", i=4, t=4),
                 in0=y_of[(block, g)][:].rearrange("p t (c i) -> p c t i", i=4),
@@ -217,10 +210,13 @@ def tile_crossattention_pb_kernel(tc, text, Wq_w, Wq_b, qn_w, k_norm, out):
                 .to_broadcast([P, BLOCK // 4, 4, 4]),
                 op=ALU.mult,
             )
+
+        def quantise_queries(block, g):
+            tokens = slice(block * BLOCK, (block + 1) * BLOCK)
             nc.vector.quantize_mx(
                 out=q_codes[:, g, tokens].bitcast(FP8X4),
                 scales=q_scales[:, g, tokens],
-                in_=q_grouped[:],
+                in_=q_grouped_of[(block, g)][:],
             )
 
         def score_pass(block, g, banks):
@@ -266,20 +262,23 @@ def tile_crossattention_pb_kernel(tc, text, Wq_w, Wq_b, qn_w, k_norm, out):
                 if block == 1 and m == 0:
                     rms_factor(0)
                 if block == 1 and m % 2 == 0:
-                    normalise(0, m // 2)
+                    scale_queries(0, m // 2)
+                if block == 1 and m % 2 == 1:
+                    quantise_queries(0, m // 2)
 
         grouped_of[FIRST_KEYS] = transpose_unit(FIRST_KEYS)
         rms_factor(1)
         for g in range(PASSES):
             if g + 1 < 4:
                 grouped_of[FIRST_KEYS + g + 1] = transpose_unit(FIRST_KEYS + g + 1)
+            scale_queries(1, g)
             quantise_unit(FIRST_KEYS + g, grouped_of[FIRST_KEYS + g])
             if g == 2:
                 banks0 = [psum.tile([P, BLOCK], F32, name="sc%d" % i, tag="mm") for i in range(4)]
                 for gg in range(PASSES):
                     score_pass(0, gg, banks0)
                 store_scores(0, banks0)
-            normalise(1, g)
+            quantise_queries(1, g)
         banks1 = [psum.tile([P, BLOCK], F32, name="sd%d" % i, tag="tp") for i in range(4)]
         for g in range(PASSES):
             score_pass(1, g, banks1)

@@ -196,11 +196,9 @@ def tile_crossattention_pb_kernel(tc, text, Wq_w, Wq_b, qn_w, k_norm, out):
             )
             inv_of[block] = inv
 
-        q_grouped_of = {}
-
-        def scale_queries(block, g):
+        def normalise(block, g):
+            tokens = slice(block * BLOCK, (block + 1) * BLOCK)
             q_grouped = q_pool.tile([P, 4 * BLOCK], BF16, name="q_grouped", align_bytes=64)
-            q_grouped_of[(block, g)] = q_grouped
             nc.vector.tensor_tensor(
                 out=q_grouped[:].rearrange("p (c i t) -> p c t i", i=4, t=4),
                 in0=y_of[(block, g)][:].rearrange("p t (c i) -> p c t i", i=4),
@@ -210,13 +208,10 @@ def tile_crossattention_pb_kernel(tc, text, Wq_w, Wq_b, qn_w, k_norm, out):
                 .to_broadcast([P, BLOCK // 4, 4, 4]),
                 op=ALU.mult,
             )
-
-        def quantise_queries(block, g):
-            tokens = slice(block * BLOCK, (block + 1) * BLOCK)
             nc.vector.quantize_mx(
                 out=q_codes[:, g, tokens].bitcast(FP8X4),
                 scales=q_scales[:, g, tokens],
-                in_=q_grouped_of[(block, g)][:],
+                in_=q_grouped[:],
             )
 
         def score_pass(block, g, banks):
@@ -262,23 +257,20 @@ def tile_crossattention_pb_kernel(tc, text, Wq_w, Wq_b, qn_w, k_norm, out):
                 if block == 1 and m == 0:
                     rms_factor(0)
                 if block == 1 and m % 2 == 0:
-                    scale_queries(0, m // 2)
-                if block == 1 and m % 2 == 1:
-                    quantise_queries(0, m // 2)
+                    normalise(0, m // 2)
 
         grouped_of[FIRST_KEYS] = transpose_unit(FIRST_KEYS)
         rms_factor(1)
         for g in range(PASSES):
             if g + 1 < 4:
                 grouped_of[FIRST_KEYS + g + 1] = transpose_unit(FIRST_KEYS + g + 1)
-            scale_queries(1, g)
             quantise_unit(FIRST_KEYS + g, grouped_of[FIRST_KEYS + g])
             if g == 2:
                 banks0 = [psum.tile([P, BLOCK], F32, name="sc%d" % i, tag="mm") for i in range(4)]
                 for gg in range(PASSES):
                     score_pass(0, gg, banks0)
                 store_scores(0, banks0)
-            quantise_queries(1, g)
+            normalise(1, g)
         banks1 = [psum.tile([P, BLOCK], F32, name="sd%d" % i, tag="tp") for i in range(4)]
         for g in range(PASSES):
             score_pass(1, g, banks1)

from contextlib import ExitStack

import concourse.mybir as mybir
from concourse.masks import make_identity

F32 = mybir.dt.float32
BF16 = mybir.dt.bfloat16
U32 = mybir.dt.uint32
U8 = mybir.dt.uint8
FP8X4 = mybir.dt.float8_e4m3fn_x4
ACT = mybir.ActivationFunctionType
ALU = mybir.AluOpType

P = 128
D = 2048
PASSES = 4
TOKENS = 1024
BLOCK = 512
UNIT_ROWS = 256
W_UNITS = D // UNIT_ROWS
EPS = 1e-6
SCORE_SCALE = 1.0 / (2048.0 ** 0.5)

FLOPS = 2 * TOKENS * D * D + 2 * TOKENS * BLOCK * D

RAW_BUFS = 4
LEAD = 4


def tile_crossattention_pb_kernel(tc, text, Wq_w, Wq_b, qn_w, k_norm, out):
    nc = tc.nc
    text_rows = text.flatten_outer_dims()
    key_rows = k_norm.flatten_outer_dims()
    out_rows = out.flatten_outer_dims()

    units = [("text", 0), ("text", 1)]
    units += [("weights", m) for m in range(W_UNITS)]
    units += [("text", 2), ("text", 3)]
    units += [("keys", h) for h in range(4)]
    FIRST_KEYS = len(units) - 4

    with ExitStack() as ctx:
        consts = ctx.enter_context(tc.tile_pool(name="consts", bufs=1))
        codes = ctx.enter_context(tc.tile_pool(name="codes", bufs=1))
        raw_pool = ctx.enter_context(tc.tile_pool(name="raw", bufs=RAW_BUFS))
        grouped_pool = ctx.enter_context(tc.tile_pool(name="grouped", bufs=3))
        y_pool = ctx.enter_context(tc.tile_pool(name="y", bufs=5))
        q_pool = ctx.enter_context(tc.tile_pool(name="q", bufs=2))
        sq_pool = ctx.enter_context(tc.tile_pool(name="sq", bufs=6))
        norm_pool = ctx.enter_context(tc.tile_pool(name="norm", bufs=2))
        o_pool = ctx.enter_context(tc.tile_pool(name="o", bufs=3))
        psum = ctx.enter_context(tc.psum_pool(name="psum", bufs=4))

        def load_unit(n):
            kind, index = units[n]
            rows = slice(index * UNIT_ROWS, (index + 1) * UNIT_ROWS)
            raw = raw_pool.tile([P, 2 * D], BF16, name="raw")
            if kind == "weights":
                view = Wq_w[rows, :].rearrange("(p e) k -> p e k", e=2)
            elif kind == "text":
                view = text_rows[rows, :].rearrange("(e p) k -> p e k", e=2)
            else:
                view = key_rows[rows, :].rearrange("(e p) k -> p e k", e=2)
            nc.sync.dma_start(out=raw[:].rearrange("p (e k) -> p e k", e=2), in_=view)
            return raw

        vec_rows = consts.tile([P, 2 * P], BF16, name="vec_rows")
        nc.vector.memset(vec_rows[:], 0.0)
        nc.scalar.dma_start(out=vec_rows[0:8, :], in_=Wq_b.rearrange("(m c) -> m c", m=8))
        nc.scalar.dma_start(out=vec_rows[8:16, :], in_=qn_w.rearrange("(m c) -> m c", m=8))

        raw_of = {}
        for n in range(RAW_BUFS):
            raw_of[n] = load_unit(n)

        ident = consts.tile([P, P], F32, name="ident")
        make_identity(nc, ident[:])
        mean_w = consts.tile([P, P], F32, name="mean_w")
        nc.vector.memset(mean_w[:], 1.0 / D)
        eps = consts.tile([P, 1], F32, name="eps")
        nc.vector.memset(eps[:], EPS)
        warm = consts.tile([P, 1], F32, name="warm")
        nc.scalar.activation(out=warm[:], in_=eps[:], func=ACT.Abs_reciprocal_sqrt)

        bias_gain = consts.tile([P, 32], F32, name="bias_gain")
        bias = bias_gain[:, 0:16]
        gain = bias_gain[:, 16:32]
        gain_bias = consts.tile([P, 16], F32, name="gain_bias")

        def spread_bias_and_gain():
            vec_bank = psum.tile([P, 2, 2, P], F32, name="tp")
            nc.tensor.transpose(vec_bank[:, 0, 0, :], vec_rows[:].bitcast(F32), ident[:])
            nc.vector.tensor_copy(out=bias_gain[:], in_=vec_bank[:, 0, 0, 0:16].bitcast(BF16))
            nc.vector.tensor_tensor(out=gain_bias[:], in0=gain, in1=bias, op=ALU.mult)

        w_codes = []
        w_scales = []
        for m in range(W_UNITS):
            w_codes.append(codes.tile([P, 2 * PASSES * P], U32, name="w_codes%d" % m, align_bytes=64))
            w_scales.append(codes.tile([P, 2 * PASSES * P], U8, name="w_scales%d" % m, align_bytes=64))
        text_codes = codes.tile([P, PASSES, TOKENS], U32, name="text_codes", align_bytes=64)
        text_scales = codes.tile([P, PASSES, TOKENS], U8, name="text_scales", align_bytes=64)
        key_codes = codes.tile([P, PASSES, TOKENS], U32, name="key_codes", align_bytes=64)
        key_scales = codes.tile([P, PASSES, TOKENS], U8, name="key_scales", align_bytes=64)
        q_codes = codes.tile([P, PASSES, TOKENS], U32, name="q_codes", align_bytes=64)
        q_scales = codes.tile([P, PASSES, TOKENS], U8, name="q_scales", align_bytes=64)

        def transpose_unit(n):
            kind, index = units[n]
            words = raw_of[n][:].bitcast(F32).rearrange(
                "p (e g u c) -> p e g u c", e=2, g=PASSES, u=2
            )
            grouped = grouped_pool.tile([P, 2 * D], BF16, name="grouped", align_bytes=64)
            grouped_words = grouped[:].bitcast(F32).rearrange(
                "p (a x r u) -> p a x r u", a=4, x=2, u=2
            )
            for a in range(4):
                bank = psum.tile([P, 2, 2, P], F32, name="tp")
                for x in range(2):
                    if kind == "weights":
                        e, g = a // 2, 2 * (a % 2) + x
                    else:
                        e, g = x, a
                    for u in range(2):
                        nc.tensor.transpose(bank[:, x, u, :], words[:, e, g, u, :], ident[:])
                nc.scalar.copy(
                    out=grouped_words[:, a], in_=bank[:].rearrange("p x u r -> p x r u")
                )
            return grouped

        def quantise_unit(n, grouped):
            kind, index = units[n]
            if kind == "weights":
                nc.vector.quantize_mx(
                    out=w_codes[index][:].bitcast(FP8X4), scales=w_scales[index][:], in_=grouped[:]
                )
                return
            dst_codes, dst_scales = (text_codes, text_scales) if kind == "text" else (key_codes, key_scales)
            cols = slice(index * UNIT_ROWS, (index + 1) * UNIT_ROWS)
            for g in range(PASSES):
                nc.vector.quantize_mx(
                    out=dst_codes[:, g, cols].bitcast(FP8X4),
                    scales=dst_scales[:, g, cols],
                    in_=grouped[:, g * 4 * UNIT_ROWS : (g + 1) * 4 * UNIT_ROWS],
                )

        y_of = {}
        acc_of = {}
        inv_of = {}

        def project(block, m):
            tokens = slice(block * BLOCK, (block + 1) * BLOCK)
            for e in range(2):
                j = 2 * m + e
                bank = psum.tile([P, BLOCK], F32, name="mm")
                for g in range(PASSES):
                    cols = slice((PASSES * e + g) * P, (PASSES * e + g + 1) * P)
                    nc.tensor.matmul_mx(
                        out=bank[:],
                        lhsT=w_codes[m][:, cols].bitcast(FP8X4),
                        lhsT_scale=w_scales[m][:, cols],
                        rhs=text_codes[:, g, tokens].bitcast(FP8X4),
                        rhs_scale=text_scales[:, g, tokens],
                        start=(g == 0),
                        stop=(g == PASSES - 1),
                    )
                if j % 4 == 0:
                    y_of[(block, j // 4)] = y_pool.tile([P, 4, BLOCK], F32, name="y4")
                y4 = y_of[(block, j // 4)]
                if j == 0:
                    acc_of[block] = norm_pool.tile([P, BLOCK], F32, name="acc")
                    sq = acc_of[block]
                else:
                    sq = sq_pool.tile([P, BLOCK], F32, name="sq")
                nc.scalar.activation(
                    out=sq[:], in_=bank[:], func=ACT.Square, bias=bias[:, j : j + 1], scale=1.0
                )
                nc.any.tensor_scalar(
                    out=y4[:, j % 4, :],
                    in0=bank[:],
                    scalar1=gain[:, j : j + 1],
                    scalar2=gain_bias[:, j : j + 1],
                    op0=ALU.mult,
                    op1=ALU.add,
                )
                if j > 0:
                    acc = acc_of[block]
                    nc.vector.tensor_tensor(out=acc[:], in0=acc[:], in1=sq[:], op=ALU.add)

        def rms_factor(block):
            bank = psum.tile([P, BLOCK], F32, name="mm")
            nc.tensor.matmul(out=bank[:], lhsT=mean_w[:], rhs=acc_of[block][:], start=True, stop=True)
            inv = norm_pool.tile([P, BLOCK], F32, name="inv")
            nc.scalar.activation(
                out=inv[:], in_=bank[:], func=ACT.Abs_reciprocal_sqrt, bias=eps[:, 0:1], scale=1.0
            )
            inv_of[block] = inv

        def normalise(block, g):
            tokens = slice(block * BLOCK, (block + 1) * BLOCK)
            q_grouped = q_pool.tile([P, 4 * BLOCK], BF16, name="q_grouped", align_bytes=64)
            nc.vector.tensor_tensor(
                out=q_grouped[:].rearrange("p (c i t) -> p c t i", i=4, t=4),
                in0=y_of[(block, g)][:].rearrange("p t (c i) -> p c t i", i=4),
                in1=inv_of[block][:]
                .rearrange("p (c i) -> p c i", i=4)
                .unsqueeze(2)
                .to_broadcast([P, BLOCK // 4, 4, 4]),
                op=ALU.mult,
            )
            nc.vector.quantize_mx(
                out=q_codes[:, g, tokens].bitcast(FP8X4),
                scales=q_scales[:, g, tokens],
                in_=q_grouped[:],
            )

        def score_pass(block, g, banks):
            keys = slice(block * BLOCK, (block + 1) * BLOCK)
            for i in range(4):
                tokens = slice(block * BLOCK + i * P, block * BLOCK + (i + 1) * P)
                nc.tensor.matmul_mx(
                    out=banks[i][:],
                    lhsT=q_codes[:, g, tokens].bitcast(FP8X4),
                    lhsT_scale=q_scales[:, g, tokens],
                    rhs=key_codes[:, g, keys].bitcast(FP8X4),
                    rhs_scale=key_scales[:, g, keys],
                    start=(g == 0),
                    stop=(g == PASSES - 1),
                )

        def store_scores(block, banks):
            for i in range(4):
                o_sb = o_pool.tile([P, BLOCK], F32, name="o_sb")
                if block == 1 and i % 2 == 1:
                    nc.vector.tensor_scalar_mul(out=o_sb[:], in0=banks[i][:], scalar1=SCORE_SCALE)
                else:
                    nc.scalar.activation(
                        out=o_sb[:], in_=banks[i][:], func=ACT.Copy, scale=SCORE_SCALE
                    )
                rows = slice(block * BLOCK + i * P, block * BLOCK + (i + 1) * P)
                nc.sync.dma_start(out=out_rows[rows, :], in_=o_sb[:])

        grouped_of = {}
        for n in range(2 * W_UNITS + LEAD):
            if 1 <= n <= FIRST_KEYS and units[n - 1][0] == "weights":
                quantise_unit(n - 1, grouped_of[n - 1])
            if n < FIRST_KEYS:
                grouped_of[n] = transpose_unit(n)
                raw_of[n + RAW_BUFS] = load_unit(n + RAW_BUFS)
                if units[n][0] == "text":
                    quantise_unit(n, grouped_of[n])
            if n == 1:
                spread_bias_and_gain()
            if n >= LEAD:
                block, m = divmod(n - LEAD, W_UNITS)
                project(block, m)
                if block == 1 and m == 0:
                    rms_factor(0)
                if block == 1 and m % 2 == 0:
                    normalise(0, m // 2)

        grouped_of[FIRST_KEYS] = transpose_unit(FIRST_KEYS)
        rms_factor(1)
        for g in range(PASSES):
            if g + 1 < 4:
                grouped_of[FIRST_KEYS + g + 1] = transpose_unit(FIRST_KEYS + g + 1)
            quantise_unit(FIRST_KEYS + g, grouped_of[FIRST_KEYS + g])
            if g == 2:
                banks0 = [psum.tile([P, BLOCK], F32, name="sc%d" % i, tag="mm") for i in range(4)]
                for gg in range(PASSES):
                    score_pass(0, gg, banks0)
                store_scores(0, banks0)
            normalise(1, g)
        banks1 = [psum.tile([P, BLOCK], F32, name="sd%d" % i, tag="tp") for i in range(4)]
        for g in range(PASSES):
            score_pass(1, g, banks1)
        store_scores(1, banks1)
